import numpy as np
import ml_dtypes

BF16 = ml_dtypes.bfloat16


def bf(x):
    return np.asarray(x, np.float32).astype(BF16)


def f32(x):
    return np.asarray(x, np.float32)


def f64(x):
    return np.asarray(x).astype(np.float64)


def striped(idx):
    return np.tile(idx.reshape(-1, 16).T, (8, 1))


C, S, N = 128, 512, 512
LN_EPS = 1e-6
PE_BASE = 10000.0


def pos_table():
    pos = np.arange(N, dtype=np.float32)[:, None]
    div = np.exp(np.arange(0, C, 2, dtype=np.float32) * np.float32(-np.log(PE_BASE) / C))
    ang = (pos * div).astype(np.float32)
    pe = np.zeros((C, N), np.float32)
    pe[0::2, :] = np.sin(ang).T
    pe[1::2, :] = np.cos(ang).T
    return pe


def setup_inputs():
    return {"embed": f32(np.random.standard_normal((C, S))), "pe": f32(pos_table()), "lnf_scale": f32(1.0 + 0.1 * np.random.standard_normal((C, 1))), "lnf_bias": f32(0.1 * np.random.standard_normal((C, 1))), "offs": striped(np.random.permutation(np.tile(np.arange(S), 2))[:N])}


def reference(embed, pe, lnf_scale, lnf_bias, offs):
    idx = offs[:16].T.reshape(-1)
    x = f64(embed)[:, idx] + f64(pe)
    mu = x.mean(axis=0, keepdims=True)
    var = np.square(x - mu).mean(axis=0, keepdims=True)
    return (x - mu) / np.sqrt(var + LN_EPS) * f64(lnf_scale) + f64(lnf_bias)

@@ -1,0 +1,67 @@
+import concourse.mybir as mybir
+
+F32 = mybir.dt.float32
+U16 = mybir.dt.uint16
+ALU = mybir.AluOpType
+FUNC = mybir.ActivationFunctionType
+
+C = 128
+S = 512
+N = 512
+LN_EPS = 1e-6
+
+FLOPS = 2 * 2 * C * C * N
+
+
+def tile_performerencoder_kernel(tc, embed, pe, lnf_scale, lnf_bias, offs, out):
+    nc = tc.nc
+    with (
+        tc.tile_pool(name="held", bufs=1) as held,
+        tc.psum_pool(name="psum", bufs=1) as psum,
+    ):
+        offsets = held.tile([C, N // 16], U16, name="offsets")
+        nc.sync.dma_start(offsets[:], offs)
+        table = held.tile([C, S], F32, name="table")
+        nc.sync.dma_start(table[:], embed)
+        place = held.tile([C, N], F32, name="place")
+        nc.scalar.dma_start(place[:], pe)
+        gain = held.tile([C, 1], F32, name="gain")
+        nc.scalar.dma_start(gain[:], lnf_scale)
+        shift = held.tile([C, 1], F32, name="shift")
+        nc.scalar.dma_start(shift[:], lnf_bias)
+
+        centre = held.tile([C, C], F32, name="centre")
+        nc.gpsimd.memset(centre[:], -1.0 / C)
+        nc.gpsimd.affine_select(
+            out=centre[:],
+            in_=centre[:],
+            compare_op=ALU.not_equal,
+            fill=1.0 - 1.0 / C,
+            base=0,
+            pattern=[[-1, C]],
+            channel_multiplier=1,
+        )
+        average = held.tile([C, C], F32, name="average")
+        nc.vector.memset(average[:], 1.0 / C)
+        eps = held.tile([C, 1], F32, name="eps")
+        nc.vector.memset(eps[:], LN_EPS)
+
+        x = held.tile([C, N], F32, name="x")
+        nc.vector.tensor_tensor(x[:], table[:].indirect(offsets[:]), place[:], ALU.add)
+
+        centred = psum.tile([C, N], F32, name="centred")
+        nc.tensor.matmul(centred[:], centre[:], x[:], start=True, stop=True)
+
+        squares = held.tile([C, N], F32, name="squares")
+        nc.scalar.activation(squares[:], centred[:], FUNC.Square)
+        var = psum.tile([C, N], F32, name="var")
+        nc.tensor.matmul(var[:], average[:], squares[:], start=True, stop=True)
+
+        rstd = held.tile([C, N], F32, name="rstd")
+        nc.scalar.activation(rstd[:], var[:], FUNC.Abs_reciprocal_sqrt, bias=eps[:])
+
+        normed = held.tile([C, N], F32, name="normed")
+        nc.vector.tensor_tensor(normed[:], centred[:], rstd[:], ALU.mult)
+        result = held.tile([C, N], F32, name="result")
+        nc.vector.tensor_scalar(result[:], normed[:], gain[:], shift[:], ALU.mult, ALU.add)
+        nc.sync.dma_start(out, result[:])

@@ -10,6 +10,9 @@ S = 512
 N = 512
 LN_EPS = 1e-6
 
+PIECES = 4
+W = N // PIECES
+
 FLOPS = 2 * 2 * C * C * N
 
 
@@ -17,18 +20,22 @@ def tile_performerencoder_kernel(tc, embed, pe, lnf_scale, lnf_bias, offs, out):
     nc = tc.nc
     with (
         tc.tile_pool(name="held", bufs=1) as held,
-        tc.psum_pool(name="psum", bufs=1) as psum,
+        tc.tile_pool(name="work", bufs=PIECES) as work,
+        tc.psum_pool(name="psum", bufs=PIECES) as psum,
     ):
         offsets = held.tile([C, N // 16], U16, name="offsets")
         nc.sync.dma_start(offsets[:], offs)
         table = held.tile([C, S], F32, name="table")
         nc.sync.dma_start(table[:], embed)
-        place = held.tile([C, N], F32, name="place")
-        nc.scalar.dma_start(place[:], pe)
+        places = []
+        for p in range(PIECES):
+            place = work.tile([C, W], F32, name="place")
+            nc.scalar.dma_start(place[:], pe[:, p * W : (p + 1) * W])
+            places.append(place)
         gain = held.tile([C, 1], F32, name="gain")
-        nc.scalar.dma_start(gain[:], lnf_scale)
+        nc.sync.dma_start(gain[:], lnf_scale)
         shift = held.tile([C, 1], F32, name="shift")
-        nc.scalar.dma_start(shift[:], lnf_bias)
+        nc.sync.dma_start(shift[:], lnf_bias)
 
         centre = held.tile([C, C], F32, name="centre")
         nc.gpsimd.memset(centre[:], -1.0 / C)
@@ -45,23 +52,35 @@ def tile_performerencoder_kernel(tc, embed, pe, lnf_scale, lnf_bias, offs, out):
         nc.vector.memset(average[:], 1.0 / C)
         eps = held.tile([C, 1], F32, name="eps")
         nc.vector.memset(eps[:], LN_EPS)
+        primed = held.tile([C, 1], F32, name="primed")
+        nc.scalar.activation(primed[:], eps[:], FUNC.Abs_reciprocal_sqrt)
 
-        x = held.tile([C, N], F32, name="x")
-        nc.vector.tensor_tensor(x[:], table[:].indirect(offsets[:]), place[:], ALU.add)
+        xs = []
+        for p in range(PIECES):
+            x = work.tile([C, W], F32, name="x")
+            picked = table[:].indirect(offsets[:, p * (W // 16) : (p + 1) * (W // 16)])
+            nc.vector.tensor_tensor(x[:], picked, places[p][:], ALU.add)
+            xs.append(x)
 
-        centred = psum.tile([C, N], F32, name="centred")
-        nc.tensor.matmul(centred[:], centre[:], x[:], start=True, stop=True)
+        centreds = []
+        for p in range(PIECES):
+            centred = psum.tile([C, W], F32, name="centred")
+            nc.tensor.matmul(centred[:], centre[:], xs[p][:], start=True, stop=True)
+            centreds.append(centred)
 
-        squares = held.tile([C, N], F32, name="squares")
-        nc.scalar.activation(squares[:], centred[:], FUNC.Square)
-        var = psum.tile([C, N], F32, name="var")
-        nc.tensor.matmul(var[:], average[:], squares[:], start=True, stop=True)
+        variances = []
+        for p in range(PIECES):
+            squares = work.tile([C, W], F32, name="squares")
+            nc.scalar.activation(squares[:], centreds[p][:], FUNC.Square)
+            var = psum.tile([C, W], F32, name="var")
+            nc.tensor.matmul(var[:], average[:], squares[:], start=True, stop=True)
+            variances.append(var)
 
-        rstd = held.tile([C, N], F32, name="rstd")
-        nc.scalar.activation(rstd[:], var[:], FUNC.Abs_reciprocal_sqrt, bias=eps[:])
-
-        normed = held.tile([C, N], F32, name="normed")
-        nc.vector.tensor_tensor(normed[:], centred[:], rstd[:], ALU.mult)
-        result = held.tile([C, N], F32, name="result")
-        nc.vector.tensor_scalar(result[:], normed[:], gain[:], shift[:], ALU.mult, ALU.add)
-        nc.sync.dma_start(out, result[:])
+        for p in range(PIECES):
+            rstd = work.tile([C, W], F32, name="rstd")
+            nc.scalar.activation(rstd[:], variances[p][:], FUNC.Abs_reciprocal_sqrt, bias=eps[:])
+            normed = work.tile([C, W], F32, name="normed")
+            nc.vector.tensor_tensor(normed[:], centreds[p][:], rstd[:], ALU.mult)
+            result = work.tile([C, W], F32, name="result")
+            nc.vector.tensor_scalar(result[:], normed[:], gain[:], shift[:], ALU.mult, ALU.add)
+            nc.sync.dma_start(out[:, p * W : (p + 1) * W], result[:])

@@ -13,6 +13,8 @@ LN_EPS = 1e-6
 PIECES = 4
 W = N // PIECES
 
+WARMING = 6
+
 FLOPS = 2 * 2 * C * C * N
 
 
@@ -21,7 +23,9 @@ def tile_performerencoder_kernel(tc, embed, pe, lnf_scale, lnf_bias, offs, out):
     with (
         tc.tile_pool(name="held", bufs=1) as held,
         tc.tile_pool(name="work", bufs=PIECES) as work,
-        tc.psum_pool(name="psum", bufs=PIECES) as psum,
+        tc.psum_pool(name="centred_banks", bufs=PIECES) as centred_banks,
+        tc.psum_pool(name="var_banks", bufs=PIECES - 1) as var_banks,
+        tc.psum_pool(name="unread_bank", bufs=1) as unread_bank,
     ):
         offsets = held.tile([C, N // 16], U16, name="offsets")
         nc.sync.dma_start(offsets[:], offs)
@@ -50,6 +54,9 @@ def tile_performerencoder_kernel(tc, embed, pe, lnf_scale, lnf_bias, offs, out):
         )
         average = held.tile([C, C], F32, name="average")
         nc.vector.memset(average[:], 1.0 / C)
+        unread = unread_bank.tile([C, C], F32, name="unread")
+        for i in range(WARMING):
+            nc.tensor.matmul(unread[:], average[:], average[:], start=True, stop=True)
         eps = held.tile([C, 1], F32, name="eps")
         nc.vector.memset(eps[:], LN_EPS)
         primed = held.tile([C, 1], F32, name="primed")
@@ -64,7 +71,7 @@ def tile_performerencoder_kernel(tc, embed, pe, lnf_scale, lnf_bias, offs, out):
 
         centreds = []
         for p in range(PIECES):
-            centred = psum.tile([C, W], F32, name="centred")
+            centred = centred_banks.tile([C, W], F32, name="centred")
             nc.tensor.matmul(centred[:], centre[:], xs[p][:], start=True, stop=True)
             centreds.append(centred)
 
@@ -72,7 +79,7 @@ def tile_performerencoder_kernel(tc, embed, pe, lnf_scale, lnf_bias, offs, out):
         for p in range(PIECES):
             squares = work.tile([C, W], F32, name="squares")
             nc.scalar.activation(squares[:], centreds[p][:], FUNC.Square)
-            var = psum.tile([C, W], F32, name="var")
+            var = var_banks.tile([C, W], F32, name="var")
             nc.tensor.matmul(var[:], average[:], squares[:], start=True, stop=True)
             variances.append(var)
 

@@ -29,12 +29,15 @@ def tile_performerencoder_kernel(tc, embed, pe, lnf_scale, lnf_bias, offs, out):
     ):
         offsets = held.tile([C, N // 16], U16, name="offsets")
         nc.sync.dma_start(offsets[:], offs)
+        queues = [nc.scalar, nc.sync]
         table = held.tile([C, S], F32, name="table")
-        nc.sync.dma_start(table[:], embed)
+        for b in range(PIECES):
+            block = slice(b * (S // PIECES), (b + 1) * (S // PIECES))
+            queues[b % 2].dma_start(table[:, block], embed[:, block])
         places = []
         for p in range(PIECES):
             place = work.tile([C, W], F32, name="place")
-            nc.scalar.dma_start(place[:], pe[:, p * W : (p + 1) * W])
+            queues[p % 2].dma_start(place[:], pe[:, p * W : (p + 1) * W])
             places.append(place)
         gain = held.tile([C, 1], F32, name="gain")
         nc.sync.dma_start(gain[:], lnf_scale)

@@ -22,23 +22,16 @@ def tile_performerencoder_kernel(tc, embed, pe, lnf_scale, lnf_bias, offs, out):
     nc = tc.nc
     with (
         tc.tile_pool(name="held", bufs=1) as held,
-        tc.tile_pool(name="work", bufs=PIECES) as work,
         tc.psum_pool(name="centred_banks", bufs=PIECES) as centred_banks,
         tc.psum_pool(name="var_banks", bufs=PIECES - 1) as var_banks,
         tc.psum_pool(name="unread_bank", bufs=1) as unread_bank,
     ):
         offsets = held.tile([C, N // 16], U16, name="offsets")
         nc.sync.dma_start(offsets[:], offs)
-        queues = [nc.scalar, nc.sync]
         table = held.tile([C, S], F32, name="table")
-        for b in range(PIECES):
-            block = slice(b * (S // PIECES), (b + 1) * (S // PIECES))
-            queues[b % 2].dma_start(table[:, block], embed[:, block])
-        places = []
-        for p in range(PIECES):
-            place = work.tile([C, W], F32, name="place")
-            queues[p % 2].dma_start(place[:], pe[:, p * W : (p + 1) * W])
-            places.append(place)
+        nc.sync.dma_start(table[:], embed)
+        place = held.tile([C, N], F32, name="place")
+        nc.scalar.dma_start(place[:], pe)
         gain = held.tile([C, 1], F32, name="gain")
         nc.sync.dma_start(gain[:], lnf_scale)
         shift = held.tile([C, 1], F32, name="shift")
@@ -65,32 +58,33 @@ def tile_performerencoder_kernel(tc, embed, pe, lnf_scale, lnf_bias, offs, out):
         primed = held.tile([C, 1], F32, name="primed")
         nc.scalar.activation(primed[:], eps[:], FUNC.Abs_reciprocal_sqrt)
 
-        xs = []
+        cols = [slice(p * W, (p + 1) * W) for p in range(PIECES)]
+        entries = [slice(p * (W // 16), (p + 1) * (W // 16)) for p in range(PIECES)]
+
+        x = held.tile([C, N], F32, name="x")
         for p in range(PIECES):
-            x = work.tile([C, W], F32, name="x")
-            picked = table[:].indirect(offsets[:, p * (W // 16) : (p + 1) * (W // 16)])
-            nc.vector.tensor_tensor(x[:], picked, places[p][:], ALU.add)
-            xs.append(x)
+            picked = table[:].indirect(offsets[:, entries[p]])
+            nc.vector.tensor_tensor(x[:, cols[p]], picked, place[:, cols[p]], ALU.add)
 
         centreds = []
         for p in range(PIECES):
             centred = centred_banks.tile([C, W], F32, name="centred")
-            nc.tensor.matmul(centred[:], centre[:], xs[p][:], start=True, stop=True)
+            nc.tensor.matmul(centred[:], centre[:], x[:, cols[p]], start=True, stop=True)
             centreds.append(centred)
 
+        squares = held.tile([C, N], F32, name="squares")
         variances = []
         for p in range(PIECES):
-            squares = work.tile([C, W], F32, name="squares")
-            nc.scalar.activation(squares[:], centreds[p][:], FUNC.Square)
+            nc.scalar.activation(squares[:, cols[p]], centreds[p][:], FUNC.Square)
             var = var_banks.tile([C, W], F32, name="var")
-            nc.tensor.matmul(var[:], average[:], squares[:], start=True, stop=True)
+            nc.tensor.matmul(var[:], average[:], squares[:, cols[p]], start=True, stop=True)
             variances.append(var)
 
+        rstd = held.tile([C, N], F32, name="rstd")
+        normed = held.tile([C, N], F32, name="normed")
+        result = held.tile([C, N], F32, name="result")
         for p in range(PIECES):
-            rstd = work.tile([C, W], F32, name="rstd")
-            nc.scalar.activation(rstd[:], variances[p][:], FUNC.Abs_reciprocal_sqrt, bias=eps[:])
-            normed = work.tile([C, W], F32, name="normed")
-            nc.vector.tensor_tensor(normed[:], centreds[p][:], rstd[:], ALU.mult)
-            result = work.tile([C, W], F32, name="result")
-            nc.vector.tensor_scalar(result[:], normed[:], gain[:], shift[:], ALU.mult, ALU.add)
-            nc.sync.dma_start(out[:, p * W : (p + 1) * W], result[:])
+            nc.scalar.activation(rstd[:, cols[p]], variances[p][:], FUNC.Abs_reciprocal_sqrt, bias=eps[:])
+            nc.vector.tensor_tensor(normed[:, cols[p]], centreds[p][:], rstd[:, cols[p]], ALU.mult)
+            nc.vector.tensor_scalar(result[:, cols[p]], normed[:, cols[p]], gain[:], shift[:], ALU.mult, ALU.add)
+            nc.sync.dma_start(out[:, cols[p]], result[:, cols[p]])

@@ -26,12 +26,17 @@ def tile_performerencoder_kernel(tc, embed, pe, lnf_scale, lnf_bias, offs, out):
         tc.psum_pool(name="var_banks", bufs=PIECES - 1) as var_banks,
         tc.psum_pool(name="unread_bank", bufs=1) as unread_bank,
     ):
+        cols = [slice(p * W, (p + 1) * W) for p in range(PIECES)]
+        entries = [slice(p * (W // 16), (p + 1) * (W // 16)) for p in range(PIECES)]
+
         offsets = held.tile([C, N // 16], U16, name="offsets")
         nc.sync.dma_start(offsets[:], offs)
         table = held.tile([C, S], F32, name="table")
         nc.sync.dma_start(table[:], embed)
         place = held.tile([C, N], F32, name="place")
-        nc.scalar.dma_start(place[:], pe)
+        nc.scalar.dma_start(place[:, cols[0]], pe[:, cols[0]])
+        for p in range(1, PIECES):
+            nc.sync.dma_start(place[:, cols[p]], pe[:, cols[p]])
         gain = held.tile([C, 1], F32, name="gain")
         nc.sync.dma_start(gain[:], lnf_scale)
         shift = held.tile([C, 1], F32, name="shift")
@@ -57,9 +62,6 @@ def tile_performerencoder_kernel(tc, embed, pe, lnf_scale, lnf_bias, offs, out):
         nc.vector.memset(eps[:], LN_EPS)
         primed = held.tile([C, 1], F32, name="primed")
         nc.scalar.activation(primed[:], eps[:], FUNC.Abs_reciprocal_sqrt)
-
-        cols = [slice(p * W, (p + 1) * W) for p in range(PIECES)]
-        entries = [slice(p * (W // 16), (p + 1) * (W // 16)) for p in range(PIECES)]
 
         x = held.tile([C, N], F32, name="x")
         for p in range(PIECES):

@@ -34,9 +34,8 @@ def tile_performerencoder_kernel(tc, embed, pe, lnf_scale, lnf_bias, offs, out):
         table = held.tile([C, S], F32, name="table")
         nc.sync.dma_start(table[:], embed)
         place = held.tile([C, N], F32, name="place")
-        nc.scalar.dma_start(place[:, cols[0]], pe[:, cols[0]])
-        for p in range(1, PIECES):
-            nc.sync.dma_start(place[:, cols[p]], pe[:, cols[p]])
+        for p in range(PIECES):
+            nc.scalar.dma_start(place[:, cols[p]], pe[:, cols[p]])
         gain = held.tile([C, 1], F32, name="gain")
         nc.sync.dma_start(gain[:], lnf_scale)
         shift = held.tile([C, 1], F32, name="shift")

@@ -13,7 +13,7 @@ LN_EPS = 1e-6
 PIECES = 4
 W = N // PIECES
 
-WARMING = 6
+WARMING = 4
 
 FLOPS = 2 * 2 * C * C * N
 
@@ -23,16 +23,15 @@ def tile_performerencoder_kernel(tc, embed, pe, lnf_scale, lnf_bias, offs, out):
     with (
         tc.tile_pool(name="held", bufs=1) as held,
         tc.psum_pool(name="centred_banks", bufs=PIECES) as centred_banks,
-        tc.psum_pool(name="var_banks", bufs=PIECES - 1) as var_banks,
-        tc.psum_pool(name="unread_bank", bufs=1) as unread_bank,
+        tc.psum_pool(name="var_banks", bufs=PIECES) as var_banks,
     ):
         cols = [slice(p * W, (p + 1) * W) for p in range(PIECES)]
         entries = [slice(p * (W // 16), (p + 1) * (W // 16)) for p in range(PIECES)]
 
-        offsets = held.tile([C, N // 16], U16, name="offsets")
-        nc.sync.dma_start(offsets[:], offs)
         table = held.tile([C, S], F32, name="table")
         nc.sync.dma_start(table[:], embed)
+        offsets = held.tile([C, N // 16], U16, name="offsets")
+        nc.sync.dma_start(offsets[:], offs)
         place = held.tile([C, N], F32, name="place")
         for p in range(PIECES):
             nc.scalar.dma_start(place[:, cols[p]], pe[:, cols[p]])
@@ -54,9 +53,9 @@ def tile_performerencoder_kernel(tc, embed, pe, lnf_scale, lnf_bias, offs, out):
         )
         average = held.tile([C, C], F32, name="average")
         nc.vector.memset(average[:], 1.0 / C)
-        unread = unread_bank.tile([C, C], F32, name="unread")
+        unread = var_banks.tile([C, W], F32, name="unread", tag="var")
         for i in range(WARMING):
-            nc.tensor.matmul(unread[:], average[:], average[:], start=True, stop=True)
+            nc.tensor.matmul(unread[:], centre[:], average[:], start=True, stop=True)
         eps = held.tile([C, 1], F32, name="eps")
         nc.vector.memset(eps[:], LN_EPS)
         primed = held.tile([C, 1], F32, name="primed")

@@ -1,6 +1,7 @@
 import concourse.mybir as mybir
 
 F32 = mybir.dt.float32
+BF16 = mybir.dt.bfloat16
 U16 = mybir.dt.uint16
 ALU = mybir.AluOpType
 FUNC = mybir.ActivationFunctionType
@@ -51,11 +52,11 @@ def tile_performerencoder_kernel(tc, embed, pe, lnf_scale, lnf_bias, offs, out):
             pattern=[[-1, C]],
             channel_multiplier=1,
         )
-        average = held.tile([C, C], F32, name="average")
+        average = held.tile([C, C], BF16, name="average")
         nc.vector.memset(average[:], 1.0 / C)
         unread = var_banks.tile([C, W], F32, name="unread", tag="var")
         for i in range(WARMING):
-            nc.tensor.matmul(unread[:], centre[:], average[:], start=True, stop=True)
+            nc.tensor.matmul(unread[:], centre[:], centre[:], start=True, stop=True)
         eps = held.tile([C, 1], F32, name="eps")
         nc.vector.memset(eps[:], LN_EPS)
         primed = held.tile([C, 1], F32, name="primed")
@@ -72,7 +73,7 @@ def tile_performerencoder_kernel(tc, embed, pe, lnf_scale, lnf_bias, offs, out):
             nc.tensor.matmul(centred[:], centre[:], x[:, cols[p]], start=True, stop=True)
             centreds.append(centred)
 
-        squares = held.tile([C, N], F32, name="squares")
+        squares = held.tile([C, N], BF16, name="squares")
         variances = []
         for p in range(PIECES):
             nc.scalar.activation(squares[:, cols[p]], centreds[p][:], FUNC.Square)

@@ -57,10 +57,8 @@ def tile_performerencoder_kernel(tc, embed, pe, lnf_scale, lnf_bias, offs, out):
         unread = var_banks.tile([C, W], F32, name="unread", tag="var")
         for i in range(WARMING):
             nc.tensor.matmul(unread[:], centre[:], centre[:], start=True, stop=True)
-        eps = held.tile([C, 1], F32, name="eps")
-        nc.vector.memset(eps[:], LN_EPS)
         primed = held.tile([C, 1], F32, name="primed")
-        nc.scalar.activation(primed[:], eps[:], FUNC.Abs_reciprocal_sqrt)
+        nc.scalar.activation(primed[:], average[:, :1], FUNC.Abs_reciprocal_sqrt)
 
         x = held.tile([C, N], F32, name="x")
         for p in range(PIECES):
@@ -85,7 +83,7 @@ def tile_performerencoder_kernel(tc, embed, pe, lnf_scale, lnf_bias, offs, out):
         normed = held.tile([C, N], F32, name="normed")
         result = held.tile([C, N], F32, name="result")
         for p in range(PIECES):
-            nc.scalar.activation(rstd[:, cols[p]], variances[p][:], FUNC.Abs_reciprocal_sqrt, bias=eps[:])
+            nc.scalar.activation(rstd[:, cols[p]], variances[p][:], FUNC.Abs_reciprocal_sqrt, bias=LN_EPS)
             nc.vector.tensor_tensor(normed[:, cols[p]], centreds[p][:], rstd[:, cols[p]], ALU.mult)
             nc.vector.tensor_scalar(result[:, cols[p]], normed[:, cols[p]], gain[:], shift[:], ALU.mult, ALU.add)
             nc.sync.dma_start(out[:, cols[p]], result[:, cols[p]])

@@ -72,18 +72,23 @@ def tile_performerencoder_kernel(tc, embed, pe, lnf_scale, lnf_bias, offs, out):
             centreds.append(centred)
 
         squares = held.tile([C, N], BF16, name="squares")
+        gained = held.tile([C, N], F32, name="gained")
         variances = []
         for p in range(PIECES):
             nc.scalar.activation(squares[:, cols[p]], centreds[p][:], FUNC.Square)
             var = var_banks.tile([C, W], F32, name="var")
             nc.tensor.matmul(var[:], average[:], squares[:, cols[p]], start=True, stop=True)
             variances.append(var)
+            nc.vector.tensor_scalar_mul(gained[:, cols[p]], centreds[p][:], gain[:])
 
         rstd = held.tile([C, N], F32, name="rstd")
         normed = held.tile([C, N], F32, name="normed")
         result = held.tile([C, N], F32, name="result")
         for p in range(PIECES):
             nc.scalar.activation(rstd[:, cols[p]], variances[p][:], FUNC.Abs_reciprocal_sqrt, bias=LN_EPS)
-            nc.vector.tensor_tensor(normed[:, cols[p]], centreds[p][:], rstd[:, cols[p]], ALU.mult)
-            nc.vector.tensor_scalar(result[:, cols[p]], normed[:, cols[p]], gain[:], shift[:], ALU.mult, ALU.add)
+            nc.vector.tensor_tensor(normed[:, cols[p]], gained[:, cols[p]], rstd[:, cols[p]], ALU.mult)
+            if p < PIECES - 1:
+                nc.vector.tensor_scalar_add(result[:, cols[p]], normed[:, cols[p]], shift[:])
+            else:
+                nc.vector.tensor_tensor(result[:, cols[p]], normed[:, cols[p]], shift[:].to_broadcast([C, W]), ALU.add)
             nc.sync.dma_start(out[:, cols[p]], result[:, cols[p]])

@@ -16,6 +16,7 @@ W = N // PIECES
 
 WARMING = 4
 
+
 FLOPS = 2 * 2 * C * C * N
 
 
@@ -36,10 +37,6 @@ def tile_performerencoder_kernel(tc, embed, pe, lnf_scale, lnf_bias, offs, out):
         place = held.tile([C, N], F32, name="place")
         for p in range(PIECES):
             nc.scalar.dma_start(place[:, cols[p]], pe[:, cols[p]])
-        gain = held.tile([C, 1], F32, name="gain")
-        nc.sync.dma_start(gain[:], lnf_scale)
-        shift = held.tile([C, 1], F32, name="shift")
-        nc.sync.dma_start(shift[:], lnf_bias)
 
         centre = held.tile([C, C], F32, name="centre")
         nc.gpsimd.memset(centre[:], -1.0 / C)
@@ -59,6 +56,11 @@ def tile_performerencoder_kernel(tc, embed, pe, lnf_scale, lnf_bias, offs, out):
             nc.tensor.matmul(unread[:], centre[:], centre[:], start=True, stop=True)
         primed = held.tile([C, 1], F32, name="primed")
         nc.scalar.activation(primed[:], average[:, :1], FUNC.Abs_reciprocal_sqrt)
+        gain = held.tile([C, 1], F32, name="gain")
+        shift = held.tile([C, 1], F32, name="shift")
+        for rows in (slice(0, C // 2), slice(C // 2, C)):
+            nc.scalar.dma_start(gain[rows, :], lnf_scale[rows, :])
+            nc.scalar.dma_start(shift[rows, :], lnf_bias[rows, :])
 
         x = held.tile([C, N], F32, name="x")
         for p in range(PIECES):

@@ -58,9 +58,9 @@ def tile_performerencoder_kernel(tc, embed, pe, lnf_scale, lnf_bias, offs, out):
         nc.scalar.activation(primed[:], average[:, :1], FUNC.Abs_reciprocal_sqrt)
         gain = held.tile([C, 1], F32, name="gain")
         shift = held.tile([C, 1], F32, name="shift")
-        for rows in (slice(0, C // 2), slice(C // 2, C)):
-            nc.scalar.dma_start(gain[rows, :], lnf_scale[rows, :])
-            nc.scalar.dma_start(shift[rows, :], lnf_bias[rows, :])
+        for tile, values in ((gain, lnf_scale), (shift, lnf_bias)):
+            for rows in (slice(0, C // 2), slice(C // 2, C)):
+                nc.scalar.dma_start(tile[rows, :], values[rows, :])
 
         x = held.tile([C, N], F32, name="x")
         for p in range(PIECES):

import concourse.mybir as mybir

F32 = mybir.dt.float32
BF16 = mybir.dt.bfloat16
U16 = mybir.dt.uint16
ALU = mybir.AluOpType
FUNC = mybir.ActivationFunctionType

C = 128
S = 512
N = 512
LN_EPS = 1e-6

PIECES = 4
W = N // PIECES

WARMING = 4


FLOPS = 2 * 2 * C * C * N


def tile_performerencoder_kernel(tc, embed, pe, lnf_scale, lnf_bias, offs, out):
    nc = tc.nc
    with (
        tc.tile_pool(name="held", bufs=1) as held,
        tc.psum_pool(name="centred_banks", bufs=PIECES) as centred_banks,
        tc.psum_pool(name="var_banks", bufs=PIECES) as var_banks,
    ):
        cols = [slice(p * W, (p + 1) * W) for p in range(PIECES)]
        entries = [slice(p * (W // 16), (p + 1) * (W // 16)) for p in range(PIECES)]

        table = held.tile([C, S], F32, name="table")
        nc.sync.dma_start(table[:], embed)
        offsets = held.tile([C, N // 16], U16, name="offsets")
        nc.sync.dma_start(offsets[:], offs)
        place = held.tile([C, N], F32, name="place")
        for p in range(PIECES):
            nc.scalar.dma_start(place[:, cols[p]], pe[:, cols[p]])

        centre = held.tile([C, C], F32, name="centre")
        nc.gpsimd.memset(centre[:], -1.0 / C)
        nc.gpsimd.affine_select(
            out=centre[:],
            in_=centre[:],
            compare_op=ALU.not_equal,
            fill=1.0 - 1.0 / C,
            base=0,
            pattern=[[-1, C]],
            channel_multiplier=1,
        )
        average = held.tile([C, C], BF16, name="average")
        nc.vector.memset(average[:], 1.0 / C)
        unread = var_banks.tile([C, W], F32, name="unread", tag="var")
        for i in range(WARMING):
            nc.tensor.matmul(unread[:], centre[:], centre[:], start=True, stop=True)
        primed = held.tile([C, 1], F32, name="primed")
        nc.scalar.activation(primed[:], average[:, :1], FUNC.Abs_reciprocal_sqrt)
        gain = held.tile([C, 1], F32, name="gain")
        shift = held.tile([C, 1], F32, name="shift")
        for tile, values in ((gain, lnf_scale), (shift, lnf_bias)):
            for rows in (slice(0, C // 2), slice(C // 2, C)):
                nc.scalar.dma_start(tile[rows, :], values[rows, :])

        x = held.tile([C, N], F32, name="x")
        for p in range(PIECES):
            picked = table[:].indirect(offsets[:, entries[p]])
            nc.vector.tensor_tensor(x[:, cols[p]], picked, place[:, cols[p]], ALU.add)

        centreds = []
        for p in range(PIECES):
            centred = centred_banks.tile([C, W], F32, name="centred")
            nc.tensor.matmul(centred[:], centre[:], x[:, cols[p]], start=True, stop=True)
            centreds.append(centred)

        squares = held.tile([C, N], BF16, name="squares")
        gained = held.tile([C, N], F32, name="gained")
        variances = []
        for p in range(PIECES):
            nc.scalar.activation(squares[:, cols[p]], centreds[p][:], FUNC.Square)
            var = var_banks.tile([C, W], F32, name="var")
            nc.tensor.matmul(var[:], average[:], squares[:, cols[p]], start=True, stop=True)
            variances.append(var)
            nc.vector.tensor_scalar_mul(gained[:, cols[p]], centreds[p][:], gain[:])

        rstd = held.tile([C, N], F32, name="rstd")
        normed = held.tile([C, N], F32, name="normed")
        result = held.tile([C, N], F32, name="result")
        for p in range(PIECES):
            nc.scalar.activation(rstd[:, cols[p]], variances[p][:], FUNC.Abs_reciprocal_sqrt, bias=LN_EPS)
            nc.vector.tensor_tensor(normed[:, cols[p]], gained[:, cols[p]], rstd[:, cols[p]], ALU.mult)
            if p < PIECES - 1:
                nc.vector.tensor_scalar_add(result[:, cols[p]], normed[:, cols[p]], shift[:])
            else:
                nc.vector.tensor_tensor(result[:, cols[p]], normed[:, cols[p]], shift[:].to_broadcast([C, W]), ALU.add)
            nc.sync.dma_start(out[:, cols[p]], result[:, cols[p]])
